import numpy as np
import ml_dtypes


def mxq(x, axis, fmt="e4m3"):
    dtype, down = {"e4m3": (ml_dtypes.float8_e4m3fn, 7), "e5m2": (ml_dtypes.float8_e5m2, 14)}[fmt]
    v = np.moveaxis(np.asarray(x, np.float32).astype(ml_dtypes.bfloat16).astype(np.float64), axis, -1)
    blocks = v.reshape(v.shape[:-1] + (-1, 32))
    amax = np.abs(blocks).max(-1, keepdims=True)
    byte = np.maximum(np.where(amax > 0, np.frexp(amax)[1] - 1 + 127, 0) - down, 1)
    scale = np.exp2(byte - 127.0)
    codes = (blocks / scale).astype(np.float32).astype(dtype).astype(np.float64)
    return np.moveaxis((codes * scale).reshape(v.shape), -1, axis)


WIDE = False


def mx_kscale(k):
    if not WIDE:
        return np.ones(k)
    levels = np.array([10, -10, 5, -5, 0])
    a = np.random.permutation(np.resize(levels, k // 512 * 4)).reshape(k // 512, 4)
    idx = np.arange(k)
    return np.exp2(a[idx // 512, idx % 128 // 32])


BF16 = ml_dtypes.bfloat16


def bf(x):
    return np.asarray(x, np.float32).astype(BF16)


def f64(x):
    return np.asarray(x).astype(np.float64)


B, S, E, H, DH, ROT, MP = 4, 2048, 512, 4, 64, 32, 2
HD = H * DH
LOC = HD // MP


def rope_sincos():
    inv_freq = 1.0 / (10000.0 ** (np.arange(0, ROT, 2) / ROT))
    ang = np.arange(S)[:, None] * inv_freq[None, :]
    return np.sin(ang), np.cos(ang)


def apply_rope(x, sin, cos):
    sin2 = np.repeat(sin, 2, axis=-1)[None, :, None, :]
    cos2 = np.repeat(cos, 2, axis=-1)[None, :, None, :]
    x1 = x[..., ::2]
    x2 = x[..., 1::2]
    rot = np.stack((-x2, x1), axis=-1).reshape(x.shape)
    return x * cos2 + rot * sin2


def setup_inputs():
    s = mx_kscale(E)
    return {"hidden_states": bf(np.random.standard_normal((B, S, E)) * s),
            "W_qkv": bf(np.random.standard_normal((3 * HD, E)) / np.sqrt(E) / s[None, :])}


def reference(hidden_states, W_qkv):
    qkv = mxq(f64(hidden_states), 2, "e4m3") @ mxq(f64(W_qkv).T, 0, "e4m3")
    qkv = qkv.reshape(B, S, MP, 3 * LOC)
    q, k, v = np.split(qkv, 3, axis=-1)
    q = q.reshape(B, S, H, DH)
    k = k.reshape(B, S, H, DH)
    v = v.reshape(B, S, H, DH)
    sin, cos = rope_sincos()
    q = np.concatenate([apply_rope(q[..., :ROT], sin, cos), q[..., ROT:]], axis=-1)
    k = np.concatenate([apply_rope(k[..., :ROT], sin, cos), k[..., ROT:]], axis=-1)
    return q, k, v

@@ -1,0 +1,285 @@
+import math
+from contextlib import ExitStack
+
+import concourse.mybir as mybir
+from concourse.masks import make_identity
+
+F32 = mybir.dt.float32
+BF16 = mybir.dt.bfloat16
+I32 = mybir.dt.int32
+U32 = mybir.dt.uint32
+U8 = mybir.dt.uint8
+FP8X4 = mybir.dt.float8_e4m3fn_x4
+ALU = mybir.AluOpType
+ACT = mybir.ActivationFunctionType
+
+P = 128
+B, S, E = 4, 2048, 512
+H, DH, ROT = 4, 64, 32
+HD = H * DH
+GROUPS = 2
+ANGLES = ROT // 2
+POS_PER_PART = S // P
+WORDS = E // 2
+CHUNK = 4
+CHUNKS = POS_PER_PART // CHUNK
+ROUND_MAGIC = 12582912.0
+
+FLOPS = 2 * B * S * E * 3 * HD
+
+
+def build_rope_tables(nc, pool, tables):
+    turns_per_position = [
+        1.0 / (2.0 * math.pi * 10000.0 ** (2.0 * j / ROT)) for j in range(ANGLES)
+    ]
+    g_hi = [round(g * 32768.0) / 32768.0 for g in turns_per_position]
+    g_lo = [g - hi for g, hi in zip(turns_per_position, g_hi)]
+
+    position_int = pool.tile([P, POS_PER_PART], I32)
+    nc.gpsimd.iota(
+        position_int[:], pattern=[[1, POS_PER_PART]], base=0, channel_multiplier=POS_PER_PART
+    )
+    position = pool.tile([P, POS_PER_PART], F32)
+    nc.vector.tensor_copy(out=position[:], in_=position_int[:])
+
+    coarse = pool.tile([P, POS_PER_PART, ANGLES], F32)
+    for j in range(ANGLES):
+        nc.vector.tensor_scalar(
+            out=coarse[:, :, j], in0=position[:], scalar1=g_hi[j], scalar2=None, op0=ALU.mult
+        )
+    coarse_integer = pool.tile([P, POS_PER_PART, ANGLES], F32)
+    nc.vector.tensor_scalar(
+        out=coarse_integer[:],
+        in0=coarse[:],
+        scalar1=ROUND_MAGIC,
+        scalar2=ROUND_MAGIC,
+        op0=ALU.add,
+        op1=ALU.subtract,
+    )
+    nc.vector.tensor_tensor(
+        out=coarse[:], in0=coarse[:], in1=coarse_integer[:], op=ALU.subtract
+    )
+    turns = pool.tile([P, POS_PER_PART, ANGLES], F32)
+    for j in range(ANGLES):
+        nc.vector.scalar_tensor_tensor(
+            out=turns[:, :, j],
+            in0=position[:],
+            scalar=g_lo[j],
+            in1=coarse[:, :, j],
+            op0=ALU.mult,
+            op1=ALU.add,
+        )
+
+    argument = pool.tile([P, 2, POS_PER_PART, ANGLES, 2], F32)
+    nc.vector.tensor_scalar_add(out=argument[:, 0, :, :, 0], in0=turns[:], scalar1=0.25)
+    nc.vector.tensor_copy(out=argument[:, 0, :, :, 1], in_=turns[:])
+    nc.vector.tensor_scalar_mul(out=argument[:, 1, :, :, 0], in0=turns[:], scalar1=-1.0)
+    nc.vector.tensor_scalar_add(out=argument[:, 1, :, :, 1], in0=turns[:], scalar1=0.25)
+    flat_argument = argument[:].rearrange("p k i j e -> p (k i j e)")
+    argument_integer = pool.tile([P, 2 * POS_PER_PART * ROT], F32)
+    nc.vector.tensor_scalar(
+        out=argument_integer[:],
+        in0=flat_argument,
+        scalar1=ROUND_MAGIC,
+        scalar2=ROUND_MAGIC,
+        op0=ALU.add,
+        op1=ALU.subtract,
+    )
+    nc.vector.tensor_tensor(
+        out=flat_argument, in0=flat_argument, in1=argument_integer[:], op=ALU.subtract
+    )
+    nc.scalar.activation(
+        out=tables[:].rearrange("p k i c -> p (k i c)"),
+        in_=flat_argument,
+        func=ACT.Sin,
+        scale=2.0 * math.pi,
+    )
+
+
+def tile_progenattention_pa_t_kernel(tc, hidden_states, W_qkv, out_0, out_1, out_2):
+    nc = tc.nc
+    with ExitStack() as ctx:
+        const = ctx.enter_context(tc.tile_pool(name="const", bufs=1))
+        x_pool = ctx.enter_context(tc.tile_pool(name="x_pool", bufs=B * CHUNKS))
+        operand_pool = ctx.enter_context(tc.tile_pool(name="operand_pool", bufs=3))
+        stage_pool = ctx.enter_context(tc.tile_pool(name="stage_pool", bufs=4))
+        psum = ctx.enter_context(tc.psum_pool(name="psum", bufs=2))
+
+        x_rows = [hidden_states[b].rearrange("(p i) k -> p (i k)", i=POS_PER_PART) for b in range(B)]
+        out_rows = [
+            [out[b].rearrange("(p i) h d -> p (i h d)", i=POS_PER_PART) for b in range(B)]
+            for out in (out_0, out_1, out_2)
+        ]
+
+        pairs = [
+            (bc, chunk, t) for bc in range(B // 2) for chunk in range(CHUNKS) for t in range(CHUNK)
+        ]
+
+        w_rows = const.tile([P, 3 * GROUPS, E], BF16)
+        nc.sync.dma_start(out=w_rows[:], in_=W_qkv.rearrange("(a p) k -> p a k", p=P))
+        x_chunks = {}
+        for bc in range(B // 2):
+            for chunk in range(CHUNKS):
+                for side in range(2):
+                    x_chunk = x_pool.tile([P, CHUNK * E], BF16)
+                    nc.sync.dma_start(
+                        out=x_chunk[:],
+                        in_=x_rows[2 * bc + side][:, chunk * CHUNK * E : (chunk + 1) * CHUNK * E],
+                    )
+                    x_chunks[(bc, chunk, side)] = x_chunk
+
+        warm_in = const.tile([P, 1], F32)
+        warm_out = const.tile([P, 1], F32)
+        nc.vector.memset(warm_in[:], 0.0)
+        nc.scalar.activation(out=warm_out[:], in_=warm_in[:], func=ACT.Sin)
+
+        tables = const.tile([P, 2, POS_PER_PART, ROT], F32)
+        build_rope_tables(nc, const, tables)
+
+        identity = const.tile([P, P], F32)
+        make_identity(nc, identity[:])
+
+        w_grouped = const.tile([P, 3 * HD * 4], BF16, align_bytes=64)
+        w_words = w_grouped[:].bitcast(F32).rearrange("p (c u) -> p c u", u=2)
+        w_codes = const.tile([P, 3 * HD], U32, align_bytes=64)
+        w_scales = const.tile([P, 3 * HD], U8, align_bytes=64)
+        for kind in range(3):
+            w_t = psum.tile([P, 2, 2, P], F32, name="transposed")
+            for g in range(GROUPS):
+                words = w_rows[:, 3 * g + kind, :].bitcast(F32)
+                for u in range(2):
+                    nc.tensor.transpose(w_t[:, g, u, :], words[:, u * P : (u + 1) * P], identity[:])
+            if kind == 2:
+                nc.scalar.copy(
+                    out=w_words[:, 2 * HD : 3 * HD, :].rearrange("p (g r) u -> p g r u", g=GROUPS),
+                    in_=w_t[:].rearrange("p g u r -> p g r u"),
+                )
+            else:
+                halves = w_t[:].rearrange("p g u (hh f d) -> p g f hh d u", hh=2, f=2)
+                for f in range(2):
+                    for g in range(GROUPS):
+                        first = f * HD + kind * (HD // 2) + g * 2 * ROT
+                        nc.scalar.copy(
+                            out=w_words[:, first : first + 2 * ROT, :].rearrange(
+                                "p (hh d) u -> p hh d u", hh=2
+                            ),
+                            in_=halves[:, g, f, :, :, :],
+                        )
+        for block in range(3):
+            nc.vector.quantize_mx(
+                out=w_codes[:, block * HD : (block + 1) * HD].bitcast(FP8X4),
+                scales=w_scales[:, block * HD : (block + 1) * HD],
+                in_=w_grouped[:, block * HD * 4 : (block + 1) * HD * 4],
+            )
+
+        def transpose_pair(bc, chunk, t):
+            transposed = psum.tile([P, 2, 2, P], F32, name="transposed")
+            for side in range(2):
+                words = x_chunks[(bc, chunk, side)][:].bitcast(F32)
+                for u in range(2):
+                    first = t * WORDS + u * P
+                    nc.tensor.transpose(
+                        transposed[:, side, u, :], words[:, first : first + P], identity[:]
+                    )
+            grouped = operand_pool.tile([P, 2 * E], BF16, align_bytes=64)
+            nc.scalar.copy(
+                out=grouped[:].bitcast(F32).rearrange("p (b r u) -> p b r u", b=2, u=2),
+                in_=transposed[:].rearrange("p b u r -> p b r u"),
+            )
+            return grouped
+
+        def quantise_pair(grouped):
+            codes = operand_pool.tile([P, 2 * P], U32, align_bytes=64)
+            scales = operand_pool.tile([P, 2 * P], U8, align_bytes=64)
+            nc.vector.quantize_mx(out=codes[:].bitcast(FP8X4), scales=scales[:], in_=grouped[:])
+            return codes, scales
+
+        def project_pair(codes, scales, qk_stage, v_stage, i, t):
+            rotated_ps = psum.tile([P, 2 * HD], F32)
+            passing_ps = psum.tile([P, 2 * HD], F32)
+            v_ps = psum.tile([P, 2 * HD], F32)
+            for block, bank in enumerate((rotated_ps, passing_ps, v_ps)):
+                for side in range(2):
+                    nc.tensor.matmul_mx(
+                        out=bank[:, side * HD : (side + 1) * HD],
+                        lhsT=codes[:, side * P : (side + 1) * P].bitcast(FP8X4),
+                        lhsT_scale=scales[:, side * P : (side + 1) * P],
+                        rhs=w_codes[:, block * HD : (block + 1) * HD].bitcast(FP8X4),
+                        rhs_scale=w_scales[:, block * HD : (block + 1) * HD],
+                        start=True,
+                        stop=True,
+                    )
+            shape = [P, 4, H, ANGLES, 2]
+            couples = rotated_ps[:].rearrange("p (c h j e) -> p c h j e", c=4, h=H, e=2)
+            spread = [
+                tables[:, k, i, :]
+                .rearrange("p (j e) -> p j e", e=2)
+                .unsqueeze(1)
+                .unsqueeze(1)
+                .to_broadcast(shape)
+                for k in range(2)
+            ]
+            rotated_out = qk_stage[:].rearrange(
+                "p b s (t h j e) -> p (b s) t h j e", t=CHUNK, h=H, e=2
+            )[:, :, t, :, 0:ANGLES, :]
+            nc.vector.tensor_tensor(
+                out=rotated_out,
+                in0=couples[:, :, :, :, 0:1].to_broadcast(shape),
+                in1=spread[0],
+                op=ALU.mult,
+            )
+            odd_product = operand_pool.tile([P, 2 * HD], F32)
+            odd_view = odd_product[:].rearrange("p (c h j e) -> p c h j e", c=4, h=H, e=2)
+            nc.vector.tensor_tensor(
+                out=odd_view,
+                in0=couples[:, :, :, :, 1:2].to_broadcast(shape),
+                in1=spread[1],
+                op=ALU.mult,
+            )
+            nc.scalar.copy(
+                out=qk_stage[:].rearrange("p b s (t h d) -> p (b s) t h d", t=CHUNK, h=H)[
+                    :, :, t, :, ROT:DH
+                ],
+                in_=passing_ps[:].rearrange("p (c h d) -> p c h d", c=4, h=H),
+            )
+            nc.scalar.copy(
+                out=v_stage[:, :, t * HD : (t + 1) * HD],
+                in_=v_ps[:].rearrange("p (b n) -> p b n", b=2),
+            )
+            return rotated_out, odd_view
+
+        def finish_pair(rotated_out, odd_view):
+            nc.vector.tensor_tensor(out=rotated_out, in0=rotated_out, in1=odd_view, op=ALU.add)
+
+        def store_chunk(bc, chunk, qk_stage, v_stage):
+            columns = slice(chunk * CHUNK * HD, (chunk + 1) * CHUNK * HD)
+            for side in range(2):
+                b = 2 * bc + side
+                nc.sync.dma_start(out=out_rows[2][b][:, columns], in_=v_stage[:, side, :])
+                nc.sync.dma_start(out=out_rows[0][b][:, columns], in_=qk_stage[:, side, 0, :])
+                nc.sync.dma_start(out=out_rows[1][b][:, columns], in_=qk_stage[:, side, 1, :])
+
+        grouped_of = {}
+        operand_of = {}
+        stage_of = {}
+        products_of = {}
+        for n in range(len(pairs) + 3):
+            if n < len(pairs):
+                grouped_of[n] = transpose_pair(*pairs[n])
+            if 0 <= n - 1 < len(pairs):
+                operand_of[n - 1] = quantise_pair(grouped_of[n - 1])
+            if 0 <= n - 2 < len(pairs):
+                bc, chunk, t = pairs[n - 2]
+                if t == 0:
+                    qk_stage = stage_pool.tile([P, 2, 2, CHUNK * HD], F32)
+                    v_stage = stage_pool.tile([P, 2, CHUNK * HD], F32)
+                    stage_of[(bc, chunk)] = (qk_stage, v_stage)
+                codes, scales = operand_of[n - 2]
+                products_of[n - 2] = project_pair(
+                    codes, scales, *stage_of[(bc, chunk)], chunk * CHUNK + t, t
+                )
+            if 0 <= n - 3:
+                bc, chunk, t = pairs[n - 3]
+                finish_pair(*products_of[n - 3])
+                if t == CHUNK - 1:
+                    store_chunk(bc, chunk, *stage_of[(bc, chunk)])

@@ -249,7 +249,7 @@ def tile_progenattention_pa_t_kernel(tc, hidden_states, W_qkv, out_0, out_1, out
             return rotated_out, odd_view
 
         def finish_pair(rotated_out, odd_view):
-            nc.vector.tensor_tensor(out=rotated_out, in0=rotated_out, in1=odd_view, op=ALU.add)
+            nc.gpsimd.tensor_tensor(out=rotated_out, in0=rotated_out, in1=odd_view, op=ALU.add)
 
         def store_chunk(bc, chunk, qk_stage, v_stage):
             columns = slice(chunk * CHUNK * HD, (chunk + 1) * CHUNK * HD)

@@ -28,7 +28,7 @@ ROUND_MAGIC = 12582912.0
 FLOPS = 2 * B * S * E * 3 * HD
 
 
-def build_rope_tables(nc, pool, tables):
+def rope_table_arguments(nc, pool):
     turns_per_position = [
         1.0 / (2.0 * math.pi * 10000.0 ** (2.0 * j / ROT)) for j in range(ANGLES)
     ]
@@ -59,7 +59,8 @@ def build_rope_tables(nc, pool, tables):
     nc.vector.tensor_tensor(
         out=coarse[:], in0=coarse[:], in1=coarse_integer[:], op=ALU.subtract
     )
-    turns = pool.tile([P, POS_PER_PART, ANGLES], F32)
+    planes = pool.tile([P, 3, POS_PER_PART * ANGLES], F32)
+    turns = planes[:, 2, :].rearrange("p (i j) -> p i j", j=ANGLES)
     for j in range(ANGLES):
         nc.vector.scalar_tensor_tensor(
             out=turns[:, :, j],
@@ -69,40 +70,30 @@ def build_rope_tables(nc, pool, tables):
             op0=ALU.mult,
             op1=ALU.add,
         )
-
-    argument = pool.tile([P, 2, POS_PER_PART, ANGLES, 2], F32)
-    nc.vector.tensor_scalar_add(out=argument[:, 0, :, :, 0], in0=turns[:], scalar1=0.25)
-    nc.vector.tensor_copy(out=argument[:, 0, :, :, 1], in_=turns[:])
-    nc.vector.tensor_scalar_mul(out=argument[:, 1, :, :, 0], in0=turns[:], scalar1=-1.0)
-    nc.vector.tensor_scalar_add(out=argument[:, 1, :, :, 1], in0=turns[:], scalar1=0.25)
-    flat_argument = argument[:].rearrange("p k i j e -> p (k i j e)")
-    argument_integer = pool.tile([P, 2 * POS_PER_PART * ROT], F32)
+    nc.vector.tensor_scalar_mul(out=planes[:, 0, :], in0=planes[:, 2, :], scalar1=-1.0)
+    nc.vector.tensor_scalar_add(out=planes[:, 1, :], in0=planes[:, 2, :], scalar1=0.25)
+    planes_integer = pool.tile([P, 3, POS_PER_PART * ANGLES], F32)
     nc.vector.tensor_scalar(
-        out=argument_integer[:],
-        in0=flat_argument,
+        out=planes_integer[:],
+        in0=planes[:],
         scalar1=ROUND_MAGIC,
         scalar2=ROUND_MAGIC,
         op0=ALU.add,
         op1=ALU.subtract,
     )
-    nc.vector.tensor_tensor(
-        out=flat_argument, in0=flat_argument, in1=argument_integer[:], op=ALU.subtract
-    )
-    nc.scalar.activation(
-        out=tables[:].rearrange("p k i c -> p (k i c)"),
-        in_=flat_argument,
-        func=ACT.Sin,
-        scale=2.0 * math.pi,
-    )
+    nc.vector.tensor_tensor(out=planes[:], in0=planes[:], in1=planes_integer[:], op=ALU.subtract)
+    return planes
 
 
 def tile_progenattention_pa_t_kernel(tc, hidden_states, W_qkv, out_0, out_1, out_2):
     nc = tc.nc
     with ExitStack() as ctx:
+        ctx.enter_context(tc.manual_schedule())
         const = ctx.enter_context(tc.tile_pool(name="const", bufs=1))
         x_pool = ctx.enter_context(tc.tile_pool(name="x_pool", bufs=B * CHUNKS))
         operand_pool = ctx.enter_context(tc.tile_pool(name="operand_pool", bufs=3))
-        stage_pool = ctx.enter_context(tc.tile_pool(name="stage_pool", bufs=4))
+        stage_pool = ctx.enter_context(tc.tile_pool(name="stage_pool", bufs=3))
+        last_stage_pool = ctx.enter_context(tc.tile_pool(name="last_stage_pool", bufs=2))
         psum = ctx.enter_context(tc.psum_pool(name="psum", bufs=2))
 
         x_rows = [hidden_states[b].rearrange("(p i) k -> p (i k)", i=POS_PER_PART) for b in range(B)]
@@ -111,30 +102,47 @@ def tile_progenattention_pa_t_kernel(tc, hidden_states, W_qkv, out_0, out_1, out
             for out in (out_0, out_1, out_2)
         ]
 
-        pairs = [
-            (bc, chunk, t) for bc in range(B // 2) for chunk in range(CHUNKS) for t in range(CHUNK)
-        ]
+        runs = [(bc, first, CHUNK) for bc in range(B // 2) for first in range(0, POS_PER_PART, CHUNK)]
+        last_bc, last_first, last_count = runs[-1]
+        half = last_count // 2
+        runs = runs[:-1] + [(last_bc, last_first, half), (last_bc, last_first + half, half)]
+        pairs = [(bc, first, count, t) for bc, first, count in runs for t in range(count)]
 
-        w_rows = const.tile([P, 3 * GROUPS, E], BF16)
-        nc.sync.dma_start(out=w_rows[:], in_=W_qkv.rearrange("(a p) k -> p a k", p=P))
+        w_rows = const.tile([P, 3, GROUPS, E], BF16)
+        w_parts = W_qkv.rearrange("(g kind p) k -> kind p g k", g=GROUPS, kind=3)
+        for kind in range(3):
+            nc.sync.dma_start(out=w_rows[:, kind, :, :], in_=w_parts[kind])
         x_chunks = {}
         for bc in range(B // 2):
             for chunk in range(CHUNKS):
                 for side in range(2):
                     x_chunk = x_pool.tile([P, CHUNK * E], BF16)
-                    nc.sync.dma_start(
-                        out=x_chunk[:],
-                        in_=x_rows[2 * bc + side][:, chunk * CHUNK * E : (chunk + 1) * CHUNK * E],
-                    )
                     x_chunks[(bc, chunk, side)] = x_chunk
+                cuts = list(range(CHUNK + 1)) if (bc, chunk) == (0, 0) else [0, CHUNK]
+                for low, high in zip(cuts[:-1], cuts[1:]):
+                    for side in range(2):
+                        nc.sync.dma_start(
+                            out=x_chunks[(bc, chunk, side)][:, low * E : high * E],
+                            in_=x_rows[2 * bc + side][
+                                :, (chunk * CHUNK + low) * E : (chunk * CHUNK + high) * E
+                            ],
+                        )
 
         warm_in = const.tile([P, 1], F32)
         warm_out = const.tile([P, 1], F32)
         nc.vector.memset(warm_in[:], 0.0)
         nc.scalar.activation(out=warm_out[:], in_=warm_in[:], func=ACT.Sin)
 
-        tables = const.tile([P, 2, POS_PER_PART, ROT], F32)
-        build_rope_tables(nc, const, tables)
+        sine_planes = rope_table_arguments(nc, const)
+        factors = const.tile([P, POS_PER_PART, 2 * ROT], F32)
+        factors_by_source = factors[:].rearrange("p i (j w e) -> p (i j) w e", w=2, e=2)
+        for w in range(2):
+            nc.scalar.activation(
+                out=factors_by_source[:, :, w, :],
+                in_=sine_planes[:, 1 - w : 3 - w, :].rearrange("p e n -> p n e"),
+                func=ACT.Sin,
+                scale=2.0 * math.pi,
+            )
 
         identity = const.tile([P, P], F32)
         make_identity(nc, identity[:])
@@ -144,9 +152,9 @@ def tile_progenattention_pa_t_kernel(tc, hidden_states, W_qkv, out_0, out_1, out
         w_codes = const.tile([P, 3 * HD], U32, align_bytes=64)
         w_scales = const.tile([P, 3 * HD], U8, align_bytes=64)
         for kind in range(3):
-            w_t = psum.tile([P, 2, 2, P], F32, name="transposed")
+            w_t = psum.tile([P, 2, 2, P], F32, name=("rotated_ps", "passing_ps", "v_ps")[kind])
             for g in range(GROUPS):
-                words = w_rows[:, 3 * g + kind, :].bitcast(F32)
+                words = w_rows[:, kind, g, :].bitcast(F32)
                 for u in range(2):
                     nc.tensor.transpose(w_t[:, g, u, :], words[:, u * P : (u + 1) * P], identity[:])
             if kind == 2:
@@ -157,14 +165,13 @@ def tile_progenattention_pa_t_kernel(tc, hidden_states, W_qkv, out_0, out_1, out
             else:
                 halves = w_t[:].rearrange("p g u (hh f d) -> p g f hh d u", hh=2, f=2)
                 for f in range(2):
-                    for g in range(GROUPS):
-                        first = f * HD + kind * (HD // 2) + g * 2 * ROT
-                        nc.scalar.copy(
-                            out=w_words[:, first : first + 2 * ROT, :].rearrange(
-                                "p (hh d) u -> p hh d u", hh=2
-                            ),
-                            in_=halves[:, g, f, :, :, :],
-                        )
+                    first_column = f * HD + kind * (HD // 2)
+                    nc.vector.tensor_copy(
+                        out=w_words[:, first_column : first_column + HD // 2, :].rearrange(
+                            "p (g hh d) u -> p g hh d u", g=GROUPS, hh=2
+                        ),
+                        in_=halves[:, :, f, :, :, :],
+                    )
         for block in range(3):
             nc.vector.quantize_mx(
                 out=w_codes[:, block * HD : (block + 1) * HD].bitcast(FP8X4),
@@ -172,14 +179,14 @@ def tile_progenattention_pa_t_kernel(tc, hidden_states, W_qkv, out_0, out_1, out
                 in_=w_grouped[:, block * HD * 4 : (block + 1) * HD * 4],
             )
 
-        def transpose_pair(bc, chunk, t):
+        def transpose_pair(bc, i):
             transposed = psum.tile([P, 2, 2, P], F32, name="transposed")
             for side in range(2):
-                words = x_chunks[(bc, chunk, side)][:].bitcast(F32)
+                words = x_chunks[(bc, i // CHUNK, side)][:].bitcast(F32)
                 for u in range(2):
-                    first = t * WORDS + u * P
+                    first_word = (i % CHUNK) * WORDS + u * P
                     nc.tensor.transpose(
-                        transposed[:, side, u, :], words[:, first : first + P], identity[:]
+                        transposed[:, side, u, :], words[:, first_word : first_word + P], identity[:]
                     )
             grouped = operand_pool.tile([P, 2 * E], BF16, align_bytes=64)
             nc.scalar.copy(
@@ -194,7 +201,7 @@ def tile_progenattention_pa_t_kernel(tc, hidden_states, W_qkv, out_0, out_1, out
             nc.vector.quantize_mx(out=codes[:].bitcast(FP8X4), scales=scales[:], in_=grouped[:])
             return codes, scales
 
-        def project_pair(codes, scales, qk_stage, v_stage, i, t):
+        def project_pair(codes, scales, qk_stage, v_stage, i, count, t):
             rotated_ps = psum.tile([P, 2 * HD], F32)
             passing_ps = psum.tile([P, 2 * HD], F32)
             v_ps = psum.tile([P, 2 * HD], F32)
@@ -209,35 +216,23 @@ def tile_progenattention_pa_t_kernel(tc, hidden_states, W_qkv, out_0, out_1, out
                         start=True,
                         stop=True,
                     )
-            shape = [P, 4, H, ANGLES, 2]
-            couples = rotated_ps[:].rearrange("p (c h j e) -> p c h j e", c=4, h=H, e=2)
-            spread = [
-                tables[:, k, i, :]
-                .rearrange("p (j e) -> p j e", e=2)
+            shape = [P, 4, H, ROT, 2]
+            products = operand_pool.tile([P, 4 * HD], F32)
+            nc.vector.tensor_tensor(
+                out=products[:].rearrange("p (c h n e) -> p c h n e", c=4, h=H, e=2),
+                in0=rotated_ps[:]
+                .rearrange("p (c h n) -> p c h n", c=4, h=H)
+                .unsqueeze(4)
+                .to_broadcast(shape),
+                in1=factors[:, i, :]
+                .rearrange("p (n e) -> p n e", e=2)
                 .unsqueeze(1)
                 .unsqueeze(1)
-                .to_broadcast(shape)
-                for k in range(2)
-            ]
-            rotated_out = qk_stage[:].rearrange(
-                "p b s (t h j e) -> p (b s) t h j e", t=CHUNK, h=H, e=2
-            )[:, :, t, :, 0:ANGLES, :]
-            nc.vector.tensor_tensor(
-                out=rotated_out,
-                in0=couples[:, :, :, :, 0:1].to_broadcast(shape),
-                in1=spread[0],
-                op=ALU.mult,
-            )
-            odd_product = operand_pool.tile([P, 2 * HD], F32)
-            odd_view = odd_product[:].rearrange("p (c h j e) -> p c h j e", c=4, h=H, e=2)
-            nc.vector.tensor_tensor(
-                out=odd_view,
-                in0=couples[:, :, :, :, 1:2].to_broadcast(shape),
-                in1=spread[1],
+                .to_broadcast(shape),
                 op=ALU.mult,
             )
             nc.scalar.copy(
-                out=qk_stage[:].rearrange("p b s (t h d) -> p (b s) t h d", t=CHUNK, h=H)[
+                out=qk_stage[:].rearrange("p b s (t h d) -> p (b s) t h d", t=count, h=H)[
                     :, :, t, :, ROT:DH
                 ],
                 in_=passing_ps[:].rearrange("p (c h d) -> p c h d", c=4, h=H),
@@ -246,18 +241,25 @@ def tile_progenattention_pa_t_kernel(tc, hidden_states, W_qkv, out_0, out_1, out
                 out=v_stage[:, :, t * HD : (t + 1) * HD],
                 in_=v_ps[:].rearrange("p (b n) -> p b n", b=2),
             )
-            return rotated_out, odd_view
+            return products
 
-        def finish_pair(rotated_out, odd_view):
-            nc.gpsimd.tensor_tensor(out=rotated_out, in0=rotated_out, in1=odd_view, op=ALU.add)
+        def finish_pair(products, qk_stage, count, t):
+            by_source = products[:].rearrange("p (c h j w e) -> p c h j w e", c=4, h=H, w=2, e=2)
+            nc.vector.tensor_tensor(
+                out=qk_stage[:].rearrange("p b s (t h j e) -> p (b s) t h j e", t=count, h=H, e=2)[
+                    :, :, t, :, 0:ANGLES, :
+                ],
+                in0=by_source[:, :, :, :, 0, :],
+                in1=by_source[:, :, :, :, 1, :],
+                op=ALU.add,
+            )
 
-        def store_chunk(bc, chunk, qk_stage, v_stage):
-            columns = slice(chunk * CHUNK * HD, (chunk + 1) * CHUNK * HD)
+        def store(kind, staged, bc, first, count):
             for side in range(2):
-                b = 2 * bc + side
-                nc.sync.dma_start(out=out_rows[2][b][:, columns], in_=v_stage[:, side, :])
-                nc.sync.dma_start(out=out_rows[0][b][:, columns], in_=qk_stage[:, side, 0, :])
-                nc.sync.dma_start(out=out_rows[1][b][:, columns], in_=qk_stage[:, side, 1, :])
+                nc.sync.dma_start(
+                    out=out_rows[kind][2 * bc + side][:, first * HD : (first + count) * HD],
+                    in_=staged[:, side, :],
+                )
 
         grouped_of = {}
         operand_of = {}
@@ -265,21 +267,28 @@ def tile_progenattention_pa_t_kernel(tc, hidden_states, W_qkv, out_0, out_1, out
         products_of = {}
         for n in range(len(pairs) + 3):
             if n < len(pairs):
-                grouped_of[n] = transpose_pair(*pairs[n])
+                bc, first, count, t = pairs[n]
+                grouped_of[n] = transpose_pair(bc, first + t)
             if 0 <= n - 1 < len(pairs):
                 operand_of[n - 1] = quantise_pair(grouped_of[n - 1])
             if 0 <= n - 2 < len(pairs):
-                bc, chunk, t = pairs[n - 2]
+                bc, first, count, t = pairs[n - 2]
                 if t == 0:
-                    qk_stage = stage_pool.tile([P, 2, 2, CHUNK * HD], F32)
-                    v_stage = stage_pool.tile([P, 2, CHUNK * HD], F32)
-                    stage_of[(bc, chunk)] = (qk_stage, v_stage)
+                    pool = stage_pool if count == CHUNK else last_stage_pool
+                    qk_stage = pool.tile([P, 2, 2, count * HD], F32)
+                    v_stage = pool.tile([P, 2, count * HD], F32)
+                    stage_of[(bc, first)] = (qk_stage, v_stage)
+                qk_stage, v_stage = stage_of[(bc, first)]
                 codes, scales = operand_of[n - 2]
                 products_of[n - 2] = project_pair(
-                    codes, scales, *stage_of[(bc, chunk)], chunk * CHUNK + t, t
+                    codes, scales, qk_stage, v_stage, first + t, count, t
                 )
+                if t == count - 1:
+                    store(2, v_stage, bc, first, count)
             if 0 <= n - 3:
-                bc, chunk, t = pairs[n - 3]
-                finish_pair(*products_of[n - 3])
-                if t == CHUNK - 1:
-                    store_chunk(bc, chunk, *stage_of[(bc, chunk)])
+                bc, first, count, t = pairs[n - 3]
+                qk_stage, v_stage = stage_of[(bc, first)]
+                finish_pair(products_of[n - 3], qk_stage, count, t)
+                if t == count - 1:
+                    for kind in range(2):
+                        store(kind, qk_stage[:, :, kind, :], bc, first, count)

import math
from contextlib import ExitStack

import concourse.mybir as mybir
from concourse.masks import make_identity

F32 = mybir.dt.float32
BF16 = mybir.dt.bfloat16
I32 = mybir.dt.int32
U32 = mybir.dt.uint32
U8 = mybir.dt.uint8
FP8X4 = mybir.dt.float8_e4m3fn_x4
ALU = mybir.AluOpType
ACT = mybir.ActivationFunctionType

P = 128
B, S, E = 4, 2048, 512
H, DH, ROT = 4, 64, 32
HD = H * DH
GROUPS = 2
ANGLES = ROT // 2
POS_PER_PART = S // P
WORDS = E // 2
CHUNK = 4
CHUNKS = POS_PER_PART // CHUNK
ROUND_MAGIC = 12582912.0

FLOPS = 2 * B * S * E * 3 * HD


def rope_table_arguments(nc, pool):
    turns_per_position = [
        1.0 / (2.0 * math.pi * 10000.0 ** (2.0 * j / ROT)) for j in range(ANGLES)
    ]
    g_hi = [round(g * 32768.0) / 32768.0 for g in turns_per_position]
    g_lo = [g - hi for g, hi in zip(turns_per_position, g_hi)]

    position_int = pool.tile([P, POS_PER_PART], I32)
    nc.gpsimd.iota(
        position_int[:], pattern=[[1, POS_PER_PART]], base=0, channel_multiplier=POS_PER_PART
    )
    position = pool.tile([P, POS_PER_PART], F32)
    nc.vector.tensor_copy(out=position[:], in_=position_int[:])

    coarse = pool.tile([P, POS_PER_PART, ANGLES], F32)
    for j in range(ANGLES):
        nc.vector.tensor_scalar(
            out=coarse[:, :, j], in0=position[:], scalar1=g_hi[j], scalar2=None, op0=ALU.mult
        )
    coarse_integer = pool.tile([P, POS_PER_PART, ANGLES], F32)
    nc.vector.tensor_scalar(
        out=coarse_integer[:],
        in0=coarse[:],
        scalar1=ROUND_MAGIC,
        scalar2=ROUND_MAGIC,
        op0=ALU.add,
        op1=ALU.subtract,
    )
    nc.vector.tensor_tensor(
        out=coarse[:], in0=coarse[:], in1=coarse_integer[:], op=ALU.subtract
    )
    planes = pool.tile([P, 3, POS_PER_PART * ANGLES], F32)
    turns = planes[:, 2, :].rearrange("p (i j) -> p i j", j=ANGLES)
    for j in range(ANGLES):
        nc.vector.scalar_tensor_tensor(
            out=turns[:, :, j],
            in0=position[:],
            scalar=g_lo[j],
            in1=coarse[:, :, j],
            op0=ALU.mult,
            op1=ALU.add,
        )
    nc.vector.tensor_scalar_mul(out=planes[:, 0, :], in0=planes[:, 2, :], scalar1=-1.0)
    nc.vector.tensor_scalar_add(out=planes[:, 1, :], in0=planes[:, 2, :], scalar1=0.25)
    planes_integer = pool.tile([P, 3, POS_PER_PART * ANGLES], F32)
    nc.vector.tensor_scalar(
        out=planes_integer[:],
        in0=planes[:],
        scalar1=ROUND_MAGIC,
        scalar2=ROUND_MAGIC,
        op0=ALU.add,
        op1=ALU.subtract,
    )
    nc.vector.tensor_tensor(out=planes[:], in0=planes[:], in1=planes_integer[:], op=ALU.subtract)
    return planes


def tile_progenattention_pa_t_kernel(tc, hidden_states, W_qkv, out_0, out_1, out_2):
    nc = tc.nc
    with ExitStack() as ctx:
        ctx.enter_context(tc.manual_schedule())
        const = ctx.enter_context(tc.tile_pool(name="const", bufs=1))
        x_pool = ctx.enter_context(tc.tile_pool(name="x_pool", bufs=B * CHUNKS))
        operand_pool = ctx.enter_context(tc.tile_pool(name="operand_pool", bufs=3))
        stage_pool = ctx.enter_context(tc.tile_pool(name="stage_pool", bufs=3))
        last_stage_pool = ctx.enter_context(tc.tile_pool(name="last_stage_pool", bufs=2))
        psum = ctx.enter_context(tc.psum_pool(name="psum", bufs=2))

        x_rows = [hidden_states[b].rearrange("(p i) k -> p (i k)", i=POS_PER_PART) for b in range(B)]
        out_rows = [
            [out[b].rearrange("(p i) h d -> p (i h d)", i=POS_PER_PART) for b in range(B)]
            for out in (out_0, out_1, out_2)
        ]

        runs = [(bc, first, CHUNK) for bc in range(B // 2) for first in range(0, POS_PER_PART, CHUNK)]
        last_bc, last_first, last_count = runs[-1]
        half = last_count // 2
        runs = runs[:-1] + [(last_bc, last_first, half), (last_bc, last_first + half, half)]
        pairs = [(bc, first, count, t) for bc, first, count in runs for t in range(count)]

        w_rows = const.tile([P, 3, GROUPS, E], BF16)
        w_parts = W_qkv.rearrange("(g kind p) k -> kind p g k", g=GROUPS, kind=3)
        for kind in range(3):
            nc.sync.dma_start(out=w_rows[:, kind, :, :], in_=w_parts[kind])
        x_chunks = {}
        for bc in range(B // 2):
            for chunk in range(CHUNKS):
                for side in range(2):
                    x_chunk = x_pool.tile([P, CHUNK * E], BF16)
                    x_chunks[(bc, chunk, side)] = x_chunk
                cuts = list(range(CHUNK + 1)) if (bc, chunk) == (0, 0) else [0, CHUNK]
                for low, high in zip(cuts[:-1], cuts[1:]):
                    for side in range(2):
                        nc.sync.dma_start(
                            out=x_chunks[(bc, chunk, side)][:, low * E : high * E],
                            in_=x_rows[2 * bc + side][
                                :, (chunk * CHUNK + low) * E : (chunk * CHUNK + high) * E
                            ],
                        )

        warm_in = const.tile([P, 1], F32)
        warm_out = const.tile([P, 1], F32)
        nc.vector.memset(warm_in[:], 0.0)
        nc.scalar.activation(out=warm_out[:], in_=warm_in[:], func=ACT.Sin)

        sine_planes = rope_table_arguments(nc, const)
        factors = const.tile([P, POS_PER_PART, 2 * ROT], F32)
        factors_by_source = factors[:].rearrange("p i (j w e) -> p (i j) w e", w=2, e=2)
        for w in range(2):
            nc.scalar.activation(
                out=factors_by_source[:, :, w, :],
                in_=sine_planes[:, 1 - w : 3 - w, :].rearrange("p e n -> p n e"),
                func=ACT.Sin,
                scale=2.0 * math.pi,
            )

        identity = const.tile([P, P], F32)
        make_identity(nc, identity[:])

        w_grouped = const.tile([P, 3 * HD * 4], BF16, align_bytes=64)
        w_words = w_grouped[:].bitcast(F32).rearrange("p (c u) -> p c u", u=2)
        w_codes = const.tile([P, 3 * HD], U32, align_bytes=64)
        w_scales = const.tile([P, 3 * HD], U8, align_bytes=64)
        for kind in range(3):
            w_t = psum.tile([P, 2, 2, P], F32, name=("rotated_ps", "passing_ps", "v_ps")[kind])
            for g in range(GROUPS):
                words = w_rows[:, kind, g, :].bitcast(F32)
                for u in range(2):
                    nc.tensor.transpose(w_t[:, g, u, :], words[:, u * P : (u + 1) * P], identity[:])
            if kind == 2:
                nc.scalar.copy(
                    out=w_words[:, 2 * HD : 3 * HD, :].rearrange("p (g r) u -> p g r u", g=GROUPS),
                    in_=w_t[:].rearrange("p g u r -> p g r u"),
                )
            else:
                halves = w_t[:].rearrange("p g u (hh f d) -> p g f hh d u", hh=2, f=2)
                for f in range(2):
                    first_column = f * HD + kind * (HD // 2)
                    nc.vector.tensor_copy(
                        out=w_words[:, first_column : first_column + HD // 2, :].rearrange(
                            "p (g hh d) u -> p g hh d u", g=GROUPS, hh=2
                        ),
                        in_=halves[:, :, f, :, :, :],
                    )
        for block in range(3):
            nc.vector.quantize_mx(
                out=w_codes[:, block * HD : (block + 1) * HD].bitcast(FP8X4),
                scales=w_scales[:, block * HD : (block + 1) * HD],
                in_=w_grouped[:, block * HD * 4 : (block + 1) * HD * 4],
            )

        def transpose_pair(bc, i):
            transposed = psum.tile([P, 2, 2, P], F32, name="transposed")
            for side in range(2):
                words = x_chunks[(bc, i // CHUNK, side)][:].bitcast(F32)
                for u in range(2):
                    first_word = (i % CHUNK) * WORDS + u * P
                    nc.tensor.transpose(
                        transposed[:, side, u, :], words[:, first_word : first_word + P], identity[:]
                    )
            grouped = operand_pool.tile([P, 2 * E], BF16, align_bytes=64)
            nc.scalar.copy(
                out=grouped[:].bitcast(F32).rearrange("p (b r u) -> p b r u", b=2, u=2),
                in_=transposed[:].rearrange("p b u r -> p b r u"),
            )
            return grouped

        def quantise_pair(grouped):
            codes = operand_pool.tile([P, 2 * P], U32, align_bytes=64)
            scales = operand_pool.tile([P, 2 * P], U8, align_bytes=64)
            nc.vector.quantize_mx(out=codes[:].bitcast(FP8X4), scales=scales[:], in_=grouped[:])
            return codes, scales

        def project_pair(codes, scales, qk_stage, v_stage, i, count, t):
            rotated_ps = psum.tile([P, 2 * HD], F32)
            passing_ps = psum.tile([P, 2 * HD], F32)
            v_ps = psum.tile([P, 2 * HD], F32)
            for block, bank in enumerate((rotated_ps, passing_ps, v_ps)):
                for side in range(2):
                    nc.tensor.matmul_mx(
                        out=bank[:, side * HD : (side + 1) * HD],
                        lhsT=codes[:, side * P : (side + 1) * P].bitcast(FP8X4),
                        lhsT_scale=scales[:, side * P : (side + 1) * P],
                        rhs=w_codes[:, block * HD : (block + 1) * HD].bitcast(FP8X4),
                        rhs_scale=w_scales[:, block * HD : (block + 1) * HD],
                        start=True,
                        stop=True,
                    )
            shape = [P, 4, H, ROT, 2]
            products = operand_pool.tile([P, 4 * HD], F32)
            nc.vector.tensor_tensor(
                out=products[:].rearrange("p (c h n e) -> p c h n e", c=4, h=H, e=2),
                in0=rotated_ps[:]
                .rearrange("p (c h n) -> p c h n", c=4, h=H)
                .unsqueeze(4)
                .to_broadcast(shape),
                in1=factors[:, i, :]
                .rearrange("p (n e) -> p n e", e=2)
                .unsqueeze(1)
                .unsqueeze(1)
                .to_broadcast(shape),
                op=ALU.mult,
            )
            nc.scalar.copy(
                out=qk_stage[:].rearrange("p b s (t h d) -> p (b s) t h d", t=count, h=H)[
                    :, :, t, :, ROT:DH
                ],
                in_=passing_ps[:].rearrange("p (c h d) -> p c h d", c=4, h=H),
            )
            nc.scalar.copy(
                out=v_stage[:, :, t * HD : (t + 1) * HD],
                in_=v_ps[:].rearrange("p (b n) -> p b n", b=2),
            )
            return products

        def finish_pair(products, qk_stage, count, t):
            by_source = products[:].rearrange("p (c h j w e) -> p c h j w e", c=4, h=H, w=2, e=2)
            nc.vector.tensor_tensor(
                out=qk_stage[:].rearrange("p b s (t h j e) -> p (b s) t h j e", t=count, h=H, e=2)[
                    :, :, t, :, 0:ANGLES, :
                ],
                in0=by_source[:, :, :, :, 0, :],
                in1=by_source[:, :, :, :, 1, :],
                op=ALU.add,
            )

        def store(kind, staged, bc, first, count):
            for side in range(2):
                nc.sync.dma_start(
                    out=out_rows[kind][2 * bc + side][:, first * HD : (first + count) * HD],
                    in_=staged[:, side, :],
                )

        grouped_of = {}
        operand_of = {}
        stage_of = {}
        products_of = {}
        for n in range(len(pairs) + 3):
            if n < len(pairs):
                bc, first, count, t = pairs[n]
                grouped_of[n] = transpose_pair(bc, first + t)
            if 0 <= n - 1 < len(pairs):
                operand_of[n - 1] = quantise_pair(grouped_of[n - 1])
            if 0 <= n - 2 < len(pairs):
                bc, first, count, t = pairs[n - 2]
                if t == 0:
                    pool = stage_pool if count == CHUNK else last_stage_pool
                    qk_stage = pool.tile([P, 2, 2, count * HD], F32)
                    v_stage = pool.tile([P, 2, count * HD], F32)
                    stage_of[(bc, first)] = (qk_stage, v_stage)
                qk_stage, v_stage = stage_of[(bc, first)]
                codes, scales = operand_of[n - 2]
                products_of[n - 2] = project_pair(
                    codes, scales, qk_stage, v_stage, first + t, count, t
                )
                if t == count - 1:
                    store(2, v_stage, bc, first, count)
            if 0 <= n - 3:
                bc, first, count, t = pairs[n - 3]
                qk_stage, v_stage = stage_of[(bc, first)]
                finish_pair(products_of[n - 3], qk_stage, count, t)
                if t == count - 1:
                    for kind in range(2):
                        store(kind, qk_stage[:, :, kind, :], bc, first, count)
